import numpy as np
import ml_dtypes


def mxq(x, axis, fmt="e4m3"):
    dtype, down = {"e4m3": (ml_dtypes.float8_e4m3fn, 7), "e5m2": (ml_dtypes.float8_e5m2, 14)}[fmt]
    v = np.moveaxis(np.asarray(x, np.float32).astype(ml_dtypes.bfloat16).astype(np.float64), axis, -1)
    blocks = v.reshape(v.shape[:-1] + (-1, 32))
    amax = np.abs(blocks).max(-1, keepdims=True)
    byte = np.maximum(np.where(amax > 0, np.frexp(amax)[1] - 1 + 127, 0) - down, 1)
    scale = np.exp2(byte - 127.0)
    codes = (blocks / scale).astype(np.float32).astype(dtype).astype(np.float64)
    return np.moveaxis((codes * scale).reshape(v.shape), -1, axis)


WIDE = False


def mx_kscale(k):
    if not WIDE:
        return np.ones(k)
    levels = np.array([10, -10, 5, -5, 0])
    a = np.random.permutation(np.resize(levels, k // 512 * 4)).reshape(k // 512, 4)
    idx = np.arange(k)
    return np.exp2(a[idx // 512, idx % 128 // 32])


BF16 = ml_dtypes.bfloat16


def bf(x):
    return np.asarray(x, np.float32).astype(BF16)


def f64(x):
    return np.asarray(x).astype(np.float64)


N, D, O, H, W = 4, 512, 512, 32, 32
K = D + D
P = H * W


def exp_softmax_pool(y):
    a = np.exp(y)
    e = np.exp(a - a.max(-1, keepdims=True))
    sm = e / e.sum(-1, keepdims=True)
    return (sm * y).sum(-1)


def setup_inputs():
    s = mx_kscale(K)
    return {"x1": bf(np.random.standard_normal((N, D, H, W)) * 0.5 * s[:D][None, :, None, None]),
            "x2": bf(np.random.standard_normal((N, D, H, W)) * 0.5 * s[D:][None, :, None, None]),
            "c1_w": bf(np.random.standard_normal((O, K)) / np.sqrt(K) / s), "c1_b": bf(np.random.standard_normal(O) * 0.3),
            "c2_w": bf(np.random.standard_normal((O, K)) / np.sqrt(K) / s), "c2_b": bf(np.random.standard_normal(O) * 0.3)}


def reference(x1, x2, c1_w, c1_b, c2_w, c2_b):
    xc = np.concatenate([f64(x1), f64(x2)], axis=1).reshape(N, K, P)
    xq = mxq(xc, 1, "e4m3")
    x1x = (mxq(f64(c1_w), 1, "e4m3") @ xq) + f64(c1_b)[None, :, None]
    x2x = (mxq(f64(c2_w), 1, "e4m3") @ xq) + f64(c2_b)[None, :, None]
    return exp_softmax_pool(x1x), exp_softmax_pool(x2x)

@@ -1,0 +1,274 @@
+from contextlib import ExitStack
+
+import concourse.mybir as mybir
+from concourse.masks import make_identity
+
+F32 = mybir.dt.float32
+BF16 = mybir.dt.bfloat16
+U32 = mybir.dt.uint32
+U8 = mybir.dt.uint8
+FP8X4 = mybir.dt.float8_e4m3fn_x4
+ACT = mybir.ActivationFunctionType
+ALU = mybir.AluOpType
+AX = mybir.AxisListType
+
+P = 128
+PACK = 4
+NB = 4
+POS = 1024
+HALF = 512
+NW = 2
+OT = 4
+NG = NB * NW * OT
+RUN = 4
+VSHARE = 352
+
+FLOPS = 2 * NW * NB * 512 * 1024 * 1024
+
+
+def tile_fr_pa_kernel(tc, x1, x2, c1_w, c1_b, c2_w, c2_b, out_0, out_1):
+    nc = tc.nc
+    xsrc = (x1, x2)
+    with ExitStack() as ctx:
+        keep = ctx.enter_context(tc.tile_pool(name="keep", bufs=1))
+        work = ctx.enter_context(tc.tile_pool(name="work", bufs=3))
+        psum = ctx.enter_context(tc.psum_pool(name="psum", bufs=8))
+        ctx.enter_context(tc.manual_schedule())
+
+        ident = keep.tile([P, P], F32, name="ident")
+        make_identity(nc, ident[:])
+        warm_in = keep.tile([P, 1], F32, name="warm_in")
+        warm_out = keep.tile([P, 1], F32, name="warm_out")
+        nc.vector.memset(warm_in[:], 0.0)
+        nc.scalar.activation(out=warm_out[:], in_=warm_in[:], func=ACT.Exp)
+        braw = keep.tile([P, P], BF16, name="braw")
+        nc.vector.memset(braw[:], 0.0)
+        result = keep.tile([P, P], F32, name="result")
+        nc.vector.memset(result[:], 0.0)
+        negm = {}
+        sume = keep.tile([P, NG], F32, name="sume")
+        sd = keep.tile([P, 2, NG], F32, name="sd")
+        junk = keep.tile([P, HALF], F32, name="junk")
+
+        wraw0 = keep.tile([P, 2, 1024], BF16, name="wraw0")
+        wraw1 = keep.tile([P, 2, 1024], BF16, name="wraw1")
+        wraw2 = keep.tile([P, 4, 1024], BF16, name="wraw2")
+        xraw = {}
+
+        def load_x(n):
+            for c in range(2):
+                t = keep.tile([P, PACK, POS], BF16, name="xraw%d%d" % (n, c))
+                nc.sync.dma_start(out=t[:], in_=xsrc[c][n].rearrange("(p j) h w -> p j (h w)", j=PACK))
+                xraw[(n, c)] = t
+
+        nc.sync.dma_start(out=wraw0[:], in_=c1_w[0:256, :].rearrange("(t p) k -> p t k", p=P))
+        nc.scalar.dma_start(out=braw[0:4, :], in_=c1_b.rearrange("(t p) -> t p", p=P))
+        nc.scalar.dma_start(out=braw[4:8, :], in_=c2_b.rearrange("(t p) -> t p", p=P))
+        load_x(0)
+        nc.sync.dma_start(out=wraw1[:], in_=c1_w[256:512, :].rearrange("(t p) k -> p t k", p=P))
+        load_x(1)
+        nc.sync.dma_start(out=wraw2[:], in_=c2_w.rearrange("(t p) k -> p t k", p=P))
+        load_x(2)
+        load_x(3)
+
+        def wrow(j):
+            if j < 2:
+                return wraw0[:, j, :].bitcast(F32)
+            if j < 4:
+                return wraw1[:, j - 2, :].bitcast(F32)
+            return wraw2[:, j - 4, :].bitcast(F32)
+
+        wq = {}
+        ws = {}
+
+        def prep_w(tiles):
+            nt = len(tiles)
+            gw = work.tile([P, nt * 1024], BF16, name="gw%d" % tiles[0], tag="gw", bufs=2, align_bytes=64)
+            codes = keep.tile([P, nt * 256], U32, name="wq%d" % tiles[0], align_bytes=64)
+            plane = keep.tile([P, nt * 256], U8, name="ws%d" % tiles[0], align_bytes=64)
+            for i, j in enumerate(tiles):
+                words = wrow(j)
+                wt = psum.tile([P, HALF], F32, name="wt%d" % j, tag="bank")
+                for c in range(2):
+                    for u in range(2):
+                        q = 2 * c + u
+                        nc.tensor.transpose(
+                            out=wt[:, q * P : (q + 1) * P],
+                            in_=words[:, 256 * c + u : 256 * c + 256 : 2],
+                            identity=ident[:],
+                        )
+                nc.scalar.copy(
+                    out=gw[:, i * 1024 : (i + 1) * 1024].bitcast(F32).rearrange("p (c o u) -> p c o u", c=2, u=2),
+                    in_=wt[:].rearrange("p (c u o) -> p c o u", c=2, u=2),
+                )
+                wq[j] = codes[:, i * 256 : (i + 1) * 256]
+                ws[j] = plane[:, i * 256 : (i + 1) * 256]
+            return gw, codes, plane
+
+        def quant_w(prepared):
+            gw, codes, plane = prepared
+            nc.vector.quantize_mx(out=codes[:].bitcast(FP8X4), scales=plane[:], in_=gw[:])
+
+        bias = keep.tile([P, 8], F32, name="bias")
+
+        def prep_bias():
+            bwide = keep.tile([P, P], F32, name="bwide")
+            nc.vector.tensor_copy(out=bwide[:], in_=braw[:])
+            bt = psum.tile([P, HALF], F32, name="bt", tag="bank")
+            nc.tensor.transpose(out=bt[:, 0:P], in_=bwide[:], identity=ident[:])
+            nc.vector.tensor_copy(out=bias[:], in_=bt[:, 0:8])
+
+        xq = {}
+        xs = {}
+        xg = {}
+
+        def new_x(n):
+            xg[n] = work.tile([P, 2, POS, PACK], BF16, name="xg%d" % n, tag="xg", bufs=1, align_bytes=64)
+            xq[n] = keep.tile([P, 2, POS], U32, name="xq%d" % n, align_bytes=64)
+            xs[n] = keep.tile([P, 2, POS], U8, name="xs%d" % n, align_bytes=64)
+
+        def views(n, c, lo, hi):
+            dst = xg[n][:, c, lo:hi, :].rearrange("p (q i) t -> p q t i", i=RUN)
+            src = xraw[(n, c)][:, :, lo:hi].rearrange("p t (q i) -> p q t i", i=RUN)
+            return dst, src
+
+        def quant_x(n, c, lo, hi):
+            nc.vector.quantize_mx(
+                out=xq[n][:, c, lo:hi].bitcast(FP8X4),
+                scales=xs[n][:, c, lo:hi],
+                in_=xg[n][:, c, lo:hi, :].rearrange("p w t -> p (w t)"),
+            )
+
+        def regroup_head(c):
+            for h in range(2):
+                dst, src = views(0, c, h * HALF, h * HALF + VSHARE)
+                nc.vector.tensor_copy(out=dst, in_=src)
+                dst, src = views(0, c, h * HALF + VSHARE, (h + 1) * HALF)
+                nc.scalar.copy(out=dst, in_=src)
+
+        def regroup_gpsimd(n):
+            for c in range(2):
+                for h in range(2):
+                    nc.gpsimd.tensor_scalar(
+                        out=xg[n][:, c, h * HALF : (h + 1) * HALF, :],
+                        in0=xraw[(n, c)][:, :, h * HALF : (h + 1) * HALF].rearrange("p t w -> p w t"),
+                        scalar1=1.0,
+                        scalar2=0.0,
+                        op0=ALU.mult,
+                        op1=ALU.add,
+                    )
+
+        ybank = {}
+        atile = {}
+        etile = {}
+
+        def column(g):
+            n, j = divmod(g, 8)
+            return (j // OT) * (NB * OT) + n * OT + j % OT
+
+        def stage_mm(g):
+            n, j = divmod(g, 8)
+            ybank[g] = [psum.tile([P, HALF], F32, name="y%d_%d" % (g, h), tag="bank") for h in range(2)]
+            for h in range(2):
+                for c in range(2):
+                    nc.tensor.matmul_mx(
+                        out=ybank[g][h][:],
+                        lhsT=wq[j][:, c * P : (c + 1) * P].bitcast(FP8X4),
+                        lhsT_scale=ws[j][:, c * P : (c + 1) * P],
+                        rhs=xq[n][:, c, h * HALF : (h + 1) * HALF].bitcast(FP8X4),
+                        rhs_scale=xs[n][:, c, h * HALF : (h + 1) * HALF],
+                        start=(c == 0),
+                        stop=(c == 1),
+                    )
+
+        def stage_a(g):
+            j = g % 8
+            atile[g] = work.tile([P, POS], F32, name="a%d" % g, tag="a")
+            for h in range(2):
+                nc.scalar.activation(
+                    out=atile[g][:, h * HALF : (h + 1) * HALF],
+                    in_=ybank[g][h][:],
+                    func=ACT.Exp,
+                    bias=bias[:, j : j + 1],
+                    scale=1.0,
+                )
+
+        def stage_b(g):
+            negm[g] = work.tile([P, 1], F32, name="negm%d" % g, tag="negm", bufs=4)
+            nc.vector.tensor_reduce(out=negm[g][:], in_=atile[g][:], axis=AX.X, op=ALU.max, negate=True)
+
+        def stage_c(g):
+            k = column(g)
+            etile[g] = work.tile([P, POS], F32, name="e%d" % g, tag="e")
+            nc.scalar.activation(
+                out=etile[g][:],
+                in_=atile[g][:],
+                func=ACT.Exp,
+                bias=negm[g][:],
+                scale=1.0,
+                accum_out=sume[:, k : k + 1],
+            )
+
+        def stage_d(g):
+            k = column(g)
+            for h in range(2):
+                nc.vector.scalar_tensor_tensor(
+                    out=junk[:],
+                    in0=ybank[g][h][:],
+                    scalar=1.0,
+                    in1=etile[g][:, h * HALF : (h + 1) * HALF],
+                    op0=ALU.mult,
+                    op1=ALU.mult,
+                    accum_out=sd[:, h, k : k + 1],
+                )
+
+        new_x(0)
+        prep_bias()
+        quant_w(prep_w([0, 1]))
+        regroup_head(0)
+        quant_x(0, 0, 0, HALF)
+        quant_x(0, 0, HALF, POS)
+        regroup_head(1)
+        quant_x(0, 1, 0, HALF)
+        quant_x(0, 1, HALF, POS)
+        quant_w(prep_w([2, 3]))
+        stage_mm(0)
+        stage_mm(1)
+        new_x(1)
+        regroup_gpsimd(1)
+
+        for i in range(NG + 2):
+            if i >= 2:
+                stage_c(i - 2)
+                stage_d(i - 2)
+            if i < NG:
+                stage_a(i)
+                stage_b(i)
+            if i in (2, 3):
+                quant_w(prep_w([2 * i, 2 * i + 1]))
+            if i % 8 == 5 and i // 8 + 1 < NB:
+                n = i // 8 + 1
+                quant_x(n, 0, 0, POS)
+                quant_x(n, 1, 0, POS)
+                if n + 1 < NB:
+                    new_x(n + 1)
+                    regroup_gpsimd(n + 1)
+            if i + 2 < NG:
+                stage_mm(i + 2)
+
+        num = keep.tile([P, NG], F32, name="num")
+        rec = keep.tile([P, NG], F32, name="rec")
+        nc.vector.reciprocal(out=rec[:], in_=sume[:])
+        nc.vector.tensor_add(out=num[:], in0=sd[:, 0, :], in1=sd[:, 1, :])
+        nc.vector.tensor_mul(out=num[:], in0=num[:], in1=rec[:])
+        nc.vector.tensor_add(
+            out=result[:, 0:NG].rearrange("p (w n t) -> p w n t", w=NW, n=NB),
+            in0=num[:].rearrange("p (w n t) -> p w n t", w=NW, n=NB),
+            in1=bias[:].rearrange("p (w t) -> p w t", w=NW).unsqueeze(2).to_broadcast([P, NW, NB, OT]),
+        )
+        rt = psum.tile([P, HALF], F32, name="rt", tag="bank")
+        nc.tensor.transpose(out=rt[:, 0:P], in_=result[:], identity=ident[:])
+        rows = keep.tile([P, P], F32, name="rows")
+        nc.vector.tensor_copy(out=rows[:], in_=rt[:, 0:P])
+        nc.sync.dma_start(out=out_0.rearrange("n (t p) -> (n t) p", p=P), in_=rows[0:16, :])
+        nc.sync.dma_start(out=out_1.rearrange("n (t p) -> (n t) p", p=P), in_=rows[16:32, :])

@@ -41,14 +41,16 @@ def tile_fr_pa_kernel(tc, x1, x2, c1_w, c1_b, c2_w, c2_b, out_0, out_1):
         warm_out = keep.tile([P, 1], F32, name="warm_out")
         nc.vector.memset(warm_in[:], 0.0)
         nc.scalar.activation(out=warm_out[:], in_=warm_in[:], func=ACT.Exp)
-        braw = keep.tile([P, P], BF16, name="braw")
-        nc.vector.memset(braw[:], 0.0)
+        braw = keep.tile([8, P], BF16, name="braw")
+        bwide = keep.tile([P, P], F32, name="bwide")
+        nc.vector.memset(bwide[:], 0.0)
         result = keep.tile([P, P], F32, name="result")
         nc.vector.memset(result[:], 0.0)
         negm = {}
         sume = keep.tile([P, NG], F32, name="sume")
         sd = keep.tile([P, 2, NG], F32, name="sd")
         junk = keep.tile([P, HALF], F32, name="junk")
+        rec = keep.tile([P, NG], F32, name="rec")
 
         wraw0 = keep.tile([P, 2, 1024], BF16, name="wraw0")
         wraw1 = keep.tile([P, 2, 1024], BF16, name="wraw1")
@@ -61,9 +63,9 @@ def tile_fr_pa_kernel(tc, x1, x2, c1_w, c1_b, c2_w, c2_b, out_0, out_1):
                 nc.sync.dma_start(out=t[:], in_=xsrc[c][n].rearrange("(p j) h w -> p j (h w)", j=PACK))
                 xraw[(n, c)] = t
 
+        nc.sync.dma_start(out=braw[0:4, :], in_=c1_b.rearrange("(t p) -> t p", p=P))
+        nc.sync.dma_start(out=braw[4:8, :], in_=c2_b.rearrange("(t p) -> t p", p=P))
         nc.sync.dma_start(out=wraw0[:], in_=c1_w[0:256, :].rearrange("(t p) k -> p t k", p=P))
-        nc.scalar.dma_start(out=braw[0:4, :], in_=c1_b.rearrange("(t p) -> t p", p=P))
-        nc.scalar.dma_start(out=braw[4:8, :], in_=c2_b.rearrange("(t p) -> t p", p=P))
         load_x(0)
         nc.sync.dma_start(out=wraw1[:], in_=c1_w[256:512, :].rearrange("(t p) k -> p t k", p=P))
         load_x(1)
@@ -112,8 +114,6 @@ def tile_fr_pa_kernel(tc, x1, x2, c1_w, c1_b, c2_w, c2_b, out_0, out_1):
         bias = keep.tile([P, 8], F32, name="bias")
 
         def prep_bias():
-            bwide = keep.tile([P, P], F32, name="bwide")
-            nc.vector.tensor_copy(out=bwide[:], in_=braw[:])
             bt = psum.tile([P, HALF], F32, name="bt", tag="bank")
             nc.tensor.transpose(out=bt[:, 0:P], in_=bwide[:], identity=ident[:])
             nc.vector.tensor_copy(out=bias[:], in_=bt[:, 0:8])
@@ -223,8 +223,9 @@ def tile_fr_pa_kernel(tc, x1, x2, c1_w, c1_b, c2_w, c2_b, out_0, out_1):
                 )
 
         new_x(0)
-        prep_bias()
+        nc.vector.tensor_copy(out=bwide[0:8, :], in_=braw[:])
         quant_w(prep_w([0, 1]))
+        prep_bias()
         regroup_head(0)
         quant_x(0, 0, 0, HALF)
         quant_x(0, 0, HALF, POS)
@@ -240,6 +241,8 @@ def tile_fr_pa_kernel(tc, x1, x2, c1_w, c1_b, c2_w, c2_b, out_0, out_1):
         for i in range(NG + 2):
             if i >= 2:
                 stage_c(i - 2)
+                if i - 2 == NG - 1:
+                    nc.vector.reciprocal(out=rec[:], in_=sume[:])
                 stage_d(i - 2)
             if i < NG:
                 stage_a(i)
@@ -257,8 +260,6 @@ def tile_fr_pa_kernel(tc, x1, x2, c1_w, c1_b, c2_w, c2_b, out_0, out_1):
                 stage_mm(i + 2)
 
         num = keep.tile([P, NG], F32, name="num")
-        rec = keep.tile([P, NG], F32, name="rec")
-        nc.vector.reciprocal(out=rec[:], in_=sume[:])
         nc.vector.tensor_add(out=num[:], in0=sd[:, 0, :], in1=sd[:, 1, :])
         nc.vector.tensor_mul(out=num[:], in0=num[:], in1=rec[:])
         nc.vector.tensor_add(

@@ -99,10 +99,12 @@ def tile_fr_pa_kernel(tc, x1, x2, c1_w, c1_b, c2_w, c2_b, out_0, out_1):
                             in_=words[:, 256 * c + u : 256 * c + 256 : 2],
                             identity=ident[:],
                         )
-                nc.scalar.copy(
-                    out=gw[:, i * 1024 : (i + 1) * 1024].bitcast(F32).rearrange("p (c o u) -> p c o u", c=2, u=2),
-                    in_=wt[:].rearrange("p (c u o) -> p c o u", c=2, u=2),
-                )
+                gw_words = gw[:, i * 1024 : (i + 1) * 1024].bitcast(F32).rearrange("p (c o u) -> p c o u", c=2, u=2)
+                wt_words = wt[:].rearrange("p (c u o) -> p c o u", c=2, u=2)
+                if j < 4:
+                    nc.scalar.copy(out=gw_words, in_=wt_words)
+                else:
+                    nc.vector.tensor_copy(out=gw_words, in_=wt_words)
                 wq[j] = codes[:, i * 256 : (i + 1) * 256]
                 ws[j] = plane[:, i * 256 : (i + 1) * 256]
             return gw, codes, plane

@@ -99,12 +99,10 @@ def tile_fr_pa_kernel(tc, x1, x2, c1_w, c1_b, c2_w, c2_b, out_0, out_1):
                             in_=words[:, 256 * c + u : 256 * c + 256 : 2],
                             identity=ident[:],
                         )
-                gw_words = gw[:, i * 1024 : (i + 1) * 1024].bitcast(F32).rearrange("p (c o u) -> p c o u", c=2, u=2)
-                wt_words = wt[:].rearrange("p (c u o) -> p c o u", c=2, u=2)
-                if j < 4:
-                    nc.scalar.copy(out=gw_words, in_=wt_words)
-                else:
-                    nc.vector.tensor_copy(out=gw_words, in_=wt_words)
+                nc.scalar.copy(
+                    out=gw[:, i * 1024 : (i + 1) * 1024].bitcast(F32).rearrange("p (c o u) -> p c o u", c=2, u=2),
+                    in_=wt[:].rearrange("p (c u o) -> p c o u", c=2, u=2),
+                )
                 wq[j] = codes[:, i * 256 : (i + 1) * 256]
                 ws[j] = plane[:, i * 256 : (i + 1) * 256]
             return gw, codes, plane
@@ -216,9 +214,9 @@ def tile_fr_pa_kernel(tc, x1, x2, c1_w, c1_b, c2_w, c2_b, out_0, out_1):
             for h in range(2):
                 nc.vector.scalar_tensor_tensor(
                     out=junk[:],
-                    in0=ybank[g][h][:],
+                    in0=etile[g][:, h * HALF : (h + 1) * HALF],
                     scalar=1.0,
-                    in1=etile[g][:, h * HALF : (h + 1) * HALF],
+                    in1=ybank[g][h][:],
                     op0=ALU.mult,
                     op1=ALU.mult,
                     accum_out=sd[:, h, k : k + 1],

@@ -21,7 +21,7 @@ NW = 2
 OT = 4
 NG = NB * NW * OT
 RUN = 4
-VSHARE = 352
+VSHARE = 296
 
 FLOPS = 2 * NW * NB * 512 * 1024 * 1024
 
@@ -32,8 +32,11 @@ def tile_fr_pa_kernel(tc, x1, x2, c1_w, c1_b, c2_w, c2_b, out_0, out_1):
     with ExitStack() as ctx:
         keep = ctx.enter_context(tc.tile_pool(name="keep", bufs=1))
         work = ctx.enter_context(tc.tile_pool(name="work", bufs=3))
-        psum = ctx.enter_context(tc.psum_pool(name="psum", bufs=8))
+        psum = ctx.enter_context(tc.psum_pool(name="psum", bufs=1))
         ctx.enter_context(tc.manual_schedule())
+
+        def bank(b, name):
+            return psum.tile([P, HALF], F32, name=name, tag="bank%d" % b)
 
         ident = keep.tile([P, P], F32, name="ident")
         make_identity(nc, ident[:])
@@ -57,21 +60,21 @@ def tile_fr_pa_kernel(tc, x1, x2, c1_w, c1_b, c2_w, c2_b, out_0, out_1):
         wraw2 = keep.tile([P, 4, 1024], BF16, name="wraw2")
         xraw = {}
 
-        def load_x(n):
-            for c in range(2):
-                t = keep.tile([P, PACK, POS], BF16, name="xraw%d%d" % (n, c))
-                nc.sync.dma_start(out=t[:], in_=xsrc[c][n].rearrange("(p j) h w -> p j (h w)", j=PACK))
-                xraw[(n, c)] = t
+        def load_x(n, c):
+            t = keep.tile([P, PACK, POS], BF16, name="xraw%d%d" % (n, c))
+            nc.sync.dma_start(out=t[:], in_=xsrc[c][n].rearrange("(p j) h w -> p j (h w)", j=PACK))
+            xraw[(n, c)] = t
 
         nc.sync.dma_start(out=braw[0:4, :], in_=c1_b.rearrange("(t p) -> t p", p=P))
         nc.sync.dma_start(out=braw[4:8, :], in_=c2_b.rearrange("(t p) -> t p", p=P))
+        load_x(0, 0)
         nc.sync.dma_start(out=wraw0[:], in_=c1_w[0:256, :].rearrange("(t p) k -> p t k", p=P))
-        load_x(0)
+        load_x(0, 1)
         nc.sync.dma_start(out=wraw1[:], in_=c1_w[256:512, :].rearrange("(t p) k -> p t k", p=P))
-        load_x(1)
         nc.sync.dma_start(out=wraw2[:], in_=c2_w.rearrange("(t p) k -> p t k", p=P))
-        load_x(2)
-        load_x(3)
+        for n in range(1, NB):
+            load_x(n, 0)
+            load_x(n, 1)
 
         def wrow(j):
             if j < 2:
@@ -83,14 +86,11 @@ def tile_fr_pa_kernel(tc, x1, x2, c1_w, c1_b, c2_w, c2_b, out_0, out_1):
         wq = {}
         ws = {}
 
-        def prep_w(tiles):
-            nt = len(tiles)
-            gw = work.tile([P, nt * 1024], BF16, name="gw%d" % tiles[0], tag="gw", bufs=2, align_bytes=64)
-            codes = keep.tile([P, nt * 256], U32, name="wq%d" % tiles[0], align_bytes=64)
-            plane = keep.tile([P, nt * 256], U8, name="ws%d" % tiles[0], align_bytes=64)
-            for i, j in enumerate(tiles):
+        def transpose_w(tiles, banks):
+            turned = []
+            for j, b in zip(tiles, banks):
                 words = wrow(j)
-                wt = psum.tile([P, HALF], F32, name="wt%d" % j, tag="bank")
+                wt = bank(b, "wt%d" % j)
                 for c in range(2):
                     for u in range(2):
                         q = 2 * c + u
@@ -99,22 +99,28 @@ def tile_fr_pa_kernel(tc, x1, x2, c1_w, c1_b, c2_w, c2_b, out_0, out_1):
                             in_=words[:, 256 * c + u : 256 * c + 256 : 2],
                             identity=ident[:],
                         )
+                turned.append(wt)
+            return tiles, turned
+
+        def finish_w(prepared):
+            tiles, turned = prepared
+            nt = len(tiles)
+            gw = work.tile([P, nt * 1024], BF16, name="gw%d" % tiles[0], tag="gw", bufs=2, align_bytes=64)
+            codes = keep.tile([P, nt * 256], U32, name="wq%d" % tiles[0], align_bytes=64)
+            plane = keep.tile([P, nt * 256], U8, name="ws%d" % tiles[0], align_bytes=64)
+            for i, j in enumerate(tiles):
                 nc.scalar.copy(
                     out=gw[:, i * 1024 : (i + 1) * 1024].bitcast(F32).rearrange("p (c o u) -> p c o u", c=2, u=2),
-                    in_=wt[:].rearrange("p (c u o) -> p c o u", c=2, u=2),
+                    in_=turned[i][:].rearrange("p (c u o) -> p c o u", c=2, u=2),
                 )
                 wq[j] = codes[:, i * 256 : (i + 1) * 256]
                 ws[j] = plane[:, i * 256 : (i + 1) * 256]
-            return gw, codes, plane
-
-        def quant_w(prepared):
-            gw, codes, plane = prepared
             nc.vector.quantize_mx(out=codes[:].bitcast(FP8X4), scales=plane[:], in_=gw[:])
 
         bias = keep.tile([P, 8], F32, name="bias")
 
         def prep_bias():
-            bt = psum.tile([P, HALF], F32, name="bt", tag="bank")
+            bt = bank(2, "bt")
             nc.tensor.transpose(out=bt[:, 0:P], in_=bwide[:], identity=ident[:])
             nc.vector.tensor_copy(out=bias[:], in_=bt[:, 0:8])
 
@@ -168,7 +174,8 @@ def tile_fr_pa_kernel(tc, x1, x2, c1_w, c1_b, c2_w, c2_b, out_0, out_1):
 
         def stage_mm(g):
             n, j = divmod(g, 8)
-            ybank[g] = [psum.tile([P, HALF], F32, name="y%d_%d" % (g, h), tag="bank") for h in range(2)]
+            pair = g if g < 4 else (1, 0, 2, 3)[g % 4]
+            ybank[g] = [bank(2 * pair + h, "y%d_%d" % (g, h)) for h in range(2)]
             for h in range(2):
                 for c in range(2):
                     nc.tensor.matmul_mx(
@@ -214,9 +221,9 @@ def tile_fr_pa_kernel(tc, x1, x2, c1_w, c1_b, c2_w, c2_b, out_0, out_1):
             for h in range(2):
                 nc.vector.scalar_tensor_tensor(
                     out=junk[:],
-                    in0=etile[g][:, h * HALF : (h + 1) * HALF],
+                    in0=ybank[g][h][:],
                     scalar=1.0,
-                    in1=ybank[g][h][:],
+                    in1=etile[g][:, h * HALF : (h + 1) * HALF],
                     op0=ALU.mult,
                     op1=ALU.mult,
                     accum_out=sd[:, h, k : k + 1],
@@ -224,17 +231,19 @@ def tile_fr_pa_kernel(tc, x1, x2, c1_w, c1_b, c2_w, c2_b, out_0, out_1):
 
         new_x(0)
         nc.vector.tensor_copy(out=bwide[0:8, :], in_=braw[:])
-        quant_w(prep_w([0, 1]))
-        prep_bias()
         regroup_head(0)
         quant_x(0, 0, 0, HALF)
         quant_x(0, 0, HALF, POS)
+        finish_w(transpose_w([0, 1], [0, 1]))
+        prep_bias()
         regroup_head(1)
         quant_x(0, 1, 0, HALF)
         quant_x(0, 1, HALF, POS)
-        quant_w(prep_w([2, 3]))
+        finish_w(transpose_w([2, 3], [4, 5]))
         stage_mm(0)
         stage_mm(1)
+        late_w = {2: transpose_w([4, 5], [6, 7])}
+        stage_mm(2)
         new_x(1)
         regroup_gpsimd(1)
 
@@ -244,11 +253,11 @@ def tile_fr_pa_kernel(tc, x1, x2, c1_w, c1_b, c2_w, c2_b, out_0, out_1):
                 if i - 2 == NG - 1:
                     nc.vector.reciprocal(out=rec[:], in_=sume[:])
                 stage_d(i - 2)
+            if i in late_w:
+                finish_w(late_w[i])
             if i < NG:
                 stage_a(i)
                 stage_b(i)
-            if i in (2, 3):
-                quant_w(prep_w([2 * i, 2 * i + 1]))
             if i % 8 == 5 and i // 8 + 1 < NB:
                 n = i // 8 + 1
                 quant_x(n, 0, 0, POS)
@@ -256,7 +265,12 @@ def tile_fr_pa_kernel(tc, x1, x2, c1_w, c1_b, c2_w, c2_b, out_0, out_1):
                 if n + 1 < NB:
                     new_x(n + 1)
                     regroup_gpsimd(n + 1)
-            if i + 2 < NG:
+            if i == 2:
+                stage_mm(3)
+                late_w[3] = transpose_w([6, 7], [0, 1])
+            if i == 3:
+                stage_mm(4)
+            if 3 <= i < NG - 2:
                 stage_mm(i + 2)
 
         num = keep.tile([P, NG], F32, name="num")
@@ -267,7 +281,7 @@ def tile_fr_pa_kernel(tc, x1, x2, c1_w, c1_b, c2_w, c2_b, out_0, out_1):
             in0=num[:].rearrange("p (w n t) -> p w n t", w=NW, n=NB),
             in1=bias[:].rearrange("p (w t) -> p w t", w=NW).unsqueeze(2).to_broadcast([P, NW, NB, OT]),
         )
-        rt = psum.tile([P, HALF], F32, name="rt", tag="bank")
+        rt = bank(0, "rt")
         nc.tensor.transpose(out=rt[:, 0:P], in_=result[:], identity=ident[:])
         rows = keep.tile([P, P], F32, name="rows")
         nc.vector.tensor_copy(out=rows[:], in_=rt[:, 0:P])

@@ -22,6 +22,14 @@ OT = 4
 NG = NB * NW * OT
 RUN = 4
 VSHARE = 296
+G_FIRST = 13
+G_LAST = 27
+BATCH = 4
+
+
+def is_g(g):
+    return g % 2 == 1 and G_FIRST <= g <= G_LAST
+
 
 FLOPS = 2 * NW * NB * 512 * 1024 * 1024
 
@@ -52,6 +60,11 @@ def tile_fr_pa_kernel(tc, x1, x2, c1_w, c1_b, c2_w, c2_b, out_0, out_1):
         negm = {}
         sume = keep.tile([P, NG], F32, name="sume")
         sd = keep.tile([P, 2, NG], F32, name="sd")
+        nc.vector.memset(sd[:], 0.0)
+        zeros = keep.tile([P, NG], F32, name="zeros")
+        nc.vector.memset(zeros[:], 0.0)
+        ones = keep.tile([P, 1], F32, name="ones")
+        nc.vector.memset(ones[:], 1.0)
         junk = keep.tile([P, HALF], F32, name="junk")
         rec = keep.tile([P, NG], F32, name="rec")
 
@@ -165,6 +178,9 @@ def tile_fr_pa_kernel(tc, x1, x2, c1_w, c1_b, c2_w, c2_b, out_0, out_1):
                     )
 
         ybank = {}
+        ysb = {}
+        prod = {}
+        acc = {}
         atile = {}
         etile = {}
 
@@ -174,7 +190,14 @@ def tile_fr_pa_kernel(tc, x1, x2, c1_w, c1_b, c2_w, c2_b, out_0, out_1):
 
         def stage_mm(g):
             n, j = divmod(g, 8)
-            pair = g if g < 4 else (1, 0, 2, 3)[g % 4]
+            if g < 4:
+                pair = g
+            elif g == NG - 1:
+                pair = 1
+            elif g % 2 == 1 and g >= G_FIRST:
+                pair = 0
+            else:
+                pair = (1, 0, 2, 3)[g % 4]
             ybank[g] = [bank(2 * pair + h, "y%d_%d" % (g, h)) for h in range(2)]
             for h in range(2):
                 for c in range(2):
@@ -188,9 +211,25 @@ def tile_fr_pa_kernel(tc, x1, x2, c1_w, c1_b, c2_w, c2_b, out_0, out_1):
                         stop=(c == 1),
                     )
 
+        def stage_copy_max(g):
+            ysb[g] = work.tile([P, POS + 2], F32, name="ysb%d" % g, tag="ysb")
+            for h in range(2):
+                nc.vector.tensor_scalar(
+                    out=ysb[g][:, h * HALF : (h + 1) * HALF],
+                    in0=ybank[g][h][:],
+                    scalar1=1.0,
+                    scalar2=None,
+                    op0=ALU.mult,
+                    op1=ALU.max,
+                    accum_out=ysb[g][:, POS + h : POS + h + 1],
+                )
+
         def stage_a(g):
             j = g % 8
-            atile[g] = work.tile([P, POS], F32, name="a%d" % g, tag="a")
+            atile[g] = work.tile([P, POS + 2], F32, name="a%d" % g, tag="a")
+            if is_g(g):
+                nc.scalar.activation(out=atile[g][:], in_=ysb[g][:], func=ACT.Exp, bias=bias[:, j : j + 1], scale=1.0)
+                return
             for h in range(2):
                 nc.scalar.activation(
                     out=atile[g][:, h * HALF : (h + 1) * HALF],
@@ -202,14 +241,15 @@ def tile_fr_pa_kernel(tc, x1, x2, c1_w, c1_b, c2_w, c2_b, out_0, out_1):
 
         def stage_b(g):
             negm[g] = work.tile([P, 1], F32, name="negm%d" % g, tag="negm", bufs=4)
-            nc.vector.tensor_reduce(out=negm[g][:], in_=atile[g][:], axis=AX.X, op=ALU.max, negate=True)
+            src = atile[g][:, POS : POS + 2] if is_g(g) else atile[g][:, 0:POS]
+            nc.vector.tensor_reduce(out=negm[g][:], in_=src, axis=AX.X, op=ALU.max, negate=True)
 
         def stage_c(g):
             k = column(g)
             etile[g] = work.tile([P, POS], F32, name="e%d" % g, tag="e")
             nc.scalar.activation(
                 out=etile[g][:],
-                in_=atile[g][:],
+                in_=atile[g][:, 0:POS],
                 func=ACT.Exp,
                 bias=negm[g][:],
                 scale=1.0,
@@ -227,6 +267,33 @@ def tile_fr_pa_kernel(tc, x1, x2, c1_w, c1_b, c2_w, c2_b, out_0, out_1):
                     op0=ALU.mult,
                     op1=ALU.mult,
                     accum_out=sd[:, h, k : k + 1],
+                )
+
+        def stage_prod(g):
+            prod[g] = work.tile([P, POS], F32, name="prod%d" % g, tag="prod")
+            nc.gpsimd.tensor_tensor(out=prod[g][:], in0=etile[g][:], in1=ysb[g][:, 0:POS], op=ALU.mult)
+
+        def stage_fold(g):
+            q = ((g - G_FIRST) // 2) % BATCH
+            if q == 0:
+                acc[0] = bank(6, "acc%d" % g)
+            for blk in range(POS // P):
+                nc.tensor.matmul(
+                    out=acc[0][:, q * P : (q + 1) * P],
+                    lhsT=prod[g][:, blk * P : (blk + 1) * P],
+                    rhs=ident[:],
+                    is_transpose=True,
+                    start=(blk == 0),
+                    stop=(blk == POS // P - 1),
+                )
+
+        def stage_finish(last):
+            accsb = work.tile([P, BATCH * P], F32, name="accsb%d" % last, tag="accsb", bufs=2)
+            nc.vector.tensor_copy(out=accsb[:], in_=acc[0][:])
+            for q in range(BATCH):
+                k = column(last - 2 * (BATCH - 1 - q))
+                nc.tensor.matmul(
+                    out=fin[:, k : k + 1], lhsT=accsb[:, q * P : (q + 1) * P], rhs=ones[:], start=True, stop=True
                 )
 
         new_x(0)
@@ -247,19 +314,36 @@ def tile_fr_pa_kernel(tc, x1, x2, c1_w, c1_b, c2_w, c2_b, out_0, out_1):
         new_x(1)
         regroup_gpsimd(1)
 
+        mm_at = {}
+        copy_at = {}
+        for g in range(5, NG):
+            at = g - 2
+            if g == NG - 1:
+                at = g - 1
+            if is_g(g) and g > G_FIRST:
+                at = g - 3
+            mm_at.setdefault(at, []).append(g)
+            if is_g(g):
+                copy_at[at + 1] = g
+        fin = None
         for i in range(NG + 2):
+            if i in copy_at:
+                stage_copy_max(copy_at[i])
             if i >= 2:
                 stage_c(i - 2)
                 if i - 2 == NG - 1:
                     nc.vector.reciprocal(out=rec[:], in_=sume[:])
-                stage_d(i - 2)
+                if is_g(i - 2):
+                    stage_prod(i - 2)
+                else:
+                    stage_d(i - 2)
             if i in late_w:
                 finish_w(late_w[i])
             if i < NG:
                 stage_a(i)
                 stage_b(i)
-            if i % 8 == 5 and i // 8 + 1 < NB:
-                n = i // 8 + 1
+            if i % 5 == 0 and 1 <= i // 5 < NB:
+                n = i // 5
                 quant_x(n, 0, 0, POS)
                 quant_x(n, 1, 0, POS)
                 if n + 1 < NB:
@@ -270,11 +354,19 @@ def tile_fr_pa_kernel(tc, x1, x2, c1_w, c1_b, c2_w, c2_b, out_0, out_1):
                 late_w[3] = transpose_w([6, 7], [0, 1])
             if i == 3:
                 stage_mm(4)
-            if 3 <= i < NG - 2:
-                stage_mm(i + 2)
+            for g in mm_at.get(i, []):
+                stage_mm(g)
+            if i == G_FIRST + 1:
+                fin = bank(7, "fin")
+                nc.tensor.matmul(out=fin[:, 0:NG], lhsT=ident[:], rhs=zeros[:], start=True, stop=True)
+            if is_g(i - 5) and ((i - 5 - G_FIRST) // 2) % BATCH == BATCH - 1:
+                stage_finish(i - 5)
+            if is_g(i - 4):
+                stage_fold(i - 4)
 
         num = keep.tile([P, NG], F32, name="num")
         nc.vector.tensor_add(out=num[:], in0=sd[:, 0, :], in1=sd[:, 1, :])
+        nc.vector.tensor_add(out=num[:], in0=num[:], in1=fin[:, 0:NG])
         nc.vector.tensor_mul(out=num[:], in0=num[:], in1=rec[:])
         nc.vector.tensor_add(
             out=result[:, 0:NG].rearrange("p (w n t) -> p w n t", w=NW, n=NB),

@@ -314,21 +314,11 @@ def tile_fr_pa_kernel(tc, x1, x2, c1_w, c1_b, c2_w, c2_b, out_0, out_1):
         new_x(1)
         regroup_gpsimd(1)
 
-        mm_at = {}
-        copy_at = {}
-        for g in range(5, NG):
-            at = g - 2
-            if g == NG - 1:
-                at = g - 1
-            if is_g(g) and g > G_FIRST:
-                at = g - 3
-            mm_at.setdefault(at, []).append(g)
-            if is_g(g):
-                copy_at[at + 1] = g
         fin = None
         for i in range(NG + 2):
-            if i in copy_at:
-                stage_copy_max(copy_at[i])
+            if is_g(i + 2) and i + 2 > G_FIRST:
+                stage_copy_max(i + 2)
+                stage_mm(i + 4)
             if i >= 2:
                 stage_c(i - 2)
                 if i - 2 == NG - 1:
@@ -337,11 +327,18 @@ def tile_fr_pa_kernel(tc, x1, x2, c1_w, c1_b, c2_w, c2_b, out_0, out_1):
                     stage_prod(i - 2)
                 else:
                     stage_d(i - 2)
+            if i == G_FIRST - 2:
+                stage_mm(G_FIRST)
+            if i == NG - 2:
+                stage_mm(NG - 1)
             if i in late_w:
                 finish_w(late_w[i])
             if i < NG:
                 stage_a(i)
                 stage_b(i)
+            if i == G_FIRST - 2:
+                stage_copy_max(G_FIRST)
+                stage_mm(G_FIRST + 2)
             if i % 5 == 0 and 1 <= i // 5 < NB:
                 n = i // 5
                 quant_x(n, 0, 0, POS)
@@ -354,8 +351,8 @@ def tile_fr_pa_kernel(tc, x1, x2, c1_w, c1_b, c2_w, c2_b, out_0, out_1):
                 late_w[3] = transpose_w([6, 7], [0, 1])
             if i == 3:
                 stage_mm(4)
-            for g in mm_at.get(i, []):
-                stage_mm(g)
+            if 3 <= i < NG - 2 and (i + 2 < G_FIRST or i % 2 == 0):
+                stage_mm(i + 2)
             if i == G_FIRST + 1:
                 fin = bank(7, "fin")
                 nc.tensor.matmul(out=fin[:, 0:NG], lhsT=ident[:], rhs=zeros[:], start=True, stop=True)

@@ -22,7 +22,7 @@ OT = 4
 NG = NB * NW * OT
 RUN = 4
 VSHARE = 296
-G_FIRST = 13
+G_FIRST = 5
 G_LAST = 27
 BATCH = 4
 
@@ -74,7 +74,7 @@ def tile_fr_pa_kernel(tc, x1, x2, c1_w, c1_b, c2_w, c2_b, out_0, out_1):
         xraw = {}
 
         def load_x(n, c):
-            t = keep.tile([P, PACK, POS], BF16, name="xraw%d%d" % (n, c))
+            t = work.tile([P, PACK, POS], BF16, name="xraw%d%d" % (n, c), tag="xraw", bufs=6)
             nc.sync.dma_start(out=t[:], in_=xsrc[c][n].rearrange("(p j) h w -> p j (h w)", j=PACK))
             xraw[(n, c)] = t
 
@@ -85,7 +85,7 @@ def tile_fr_pa_kernel(tc, x1, x2, c1_w, c1_b, c2_w, c2_b, out_0, out_1):
         load_x(0, 1)
         nc.sync.dma_start(out=wraw1[:], in_=c1_w[256:512, :].rearrange("(t p) k -> p t k", p=P))
         nc.sync.dma_start(out=wraw2[:], in_=c2_w.rearrange("(t p) k -> p t k", p=P))
-        for n in range(1, NB):
+        for n in range(1, NB - 1):
             load_x(n, 0)
             load_x(n, 1)
 
@@ -142,7 +142,7 @@ def tile_fr_pa_kernel(tc, x1, x2, c1_w, c1_b, c2_w, c2_b, out_0, out_1):
         xg = {}
 
         def new_x(n):
-            xg[n] = work.tile([P, 2, POS, PACK], BF16, name="xg%d" % n, tag="xg", bufs=1, align_bytes=64)
+            xg[n] = work.tile([P, 2, POS, PACK], BF16, name="xg%d" % n, tag="xg", bufs=2, align_bytes=64)
             xq[n] = keep.tile([P, 2, POS], U32, name="xq%d" % n, align_bytes=64)
             xs[n] = keep.tile([P, 2, POS], U8, name="xs%d" % n, align_bytes=64)
 
@@ -165,17 +165,15 @@ def tile_fr_pa_kernel(tc, x1, x2, c1_w, c1_b, c2_w, c2_b, out_0, out_1):
                 dst, src = views(0, c, h * HALF + VSHARE, (h + 1) * HALF)
                 nc.scalar.copy(out=dst, in_=src)
 
-        def regroup_gpsimd(n):
-            for c in range(2):
-                for h in range(2):
-                    nc.gpsimd.tensor_scalar(
-                        out=xg[n][:, c, h * HALF : (h + 1) * HALF, :],
-                        in0=xraw[(n, c)][:, :, h * HALF : (h + 1) * HALF].rearrange("p t w -> p w t"),
-                        scalar1=1.0,
-                        scalar2=0.0,
-                        op0=ALU.mult,
-                        op1=ALU.add,
-                    )
+        def regroup_gpsimd(n, c, h):
+            nc.gpsimd.tensor_scalar(
+                out=xg[n][:, c, h * HALF : (h + 1) * HALF, :],
+                in0=xraw[(n, c)][:, :, h * HALF : (h + 1) * HALF].rearrange("p t w -> p w t"),
+                scalar1=1.0,
+                scalar2=0.0,
+                op0=ALU.mult,
+                op1=ALU.add,
+            )
 
         ybank = {}
         ysb = {}
@@ -212,7 +210,7 @@ def tile_fr_pa_kernel(tc, x1, x2, c1_w, c1_b, c2_w, c2_b, out_0, out_1):
                     )
 
         def stage_copy_max(g):
-            ysb[g] = work.tile([P, POS + 2], F32, name="ysb%d" % g, tag="ysb")
+            ysb[g] = work.tile([P, POS + 2], F32, name="ysb%d" % g, tag="ysb", bufs=4)
             for h in range(2):
                 nc.vector.tensor_scalar(
                     out=ysb[g][:, h * HALF : (h + 1) * HALF],
@@ -311,14 +309,18 @@ def tile_fr_pa_kernel(tc, x1, x2, c1_w, c1_b, c2_w, c2_b, out_0, out_1):
         stage_mm(1)
         late_w = {2: transpose_w([4, 5], [6, 7])}
         stage_mm(2)
+        load_x(NB - 1, 0)
+        load_x(NB - 1, 1)
         new_x(1)
-        regroup_gpsimd(1)
+        for c in range(2):
+            for h in range(2):
+                regroup_gpsimd(1, c, h)
+        pieces = [(n, c, h) for n in range(2, NB) for c in range(2) for h in range(2)]
 
         fin = None
         for i in range(NG + 2):
             if is_g(i + 2) and i + 2 > G_FIRST:
                 stage_copy_max(i + 2)
-                stage_mm(i + 4)
             if i >= 2:
                 stage_c(i - 2)
                 if i - 2 == NG - 1:
@@ -327,30 +329,31 @@ def tile_fr_pa_kernel(tc, x1, x2, c1_w, c1_b, c2_w, c2_b, out_0, out_1):
                     stage_prod(i - 2)
                 else:
                     stage_d(i - 2)
-            if i == G_FIRST - 2:
-                stage_mm(G_FIRST)
             if i == NG - 2:
                 stage_mm(NG - 1)
             if i in late_w:
                 finish_w(late_w[i])
+            if i == G_FIRST - 2:
+                stage_mm(G_FIRST)
             if i < NG:
                 stage_a(i)
                 stage_b(i)
             if i == G_FIRST - 2:
                 stage_copy_max(G_FIRST)
-                stage_mm(G_FIRST + 2)
-            if i % 5 == 0 and 1 <= i // 5 < NB:
-                n = i // 5
-                quant_x(n, 0, 0, POS)
-                quant_x(n, 1, 0, POS)
-                if n + 1 < NB:
-                    new_x(n + 1)
-                    regroup_gpsimd(n + 1)
+            if i % 8 in (3, 5) and i // 8 + 1 < NB:
+                quant_x(i // 8 + 1, (i % 8 - 3) // 2, 0, POS)
+            if i % 2 == 0 and 0 <= (i - 4) // 2 < len(pieces):
+                n, c, h = pieces[(i - 4) // 2]
+                if c == 0 and h == 0:
+                    new_x(n)
+                regroup_gpsimd(n, c, h)
             if i == 2:
                 stage_mm(3)
                 late_w[3] = transpose_w([6, 7], [0, 1])
             if i == 3:
                 stage_mm(4)
+            if i % 2 == 0 and G_FIRST < i + 3 < NG - 1:
+                stage_mm(i + 3)
             if 3 <= i < NG - 2 and (i + 2 < G_FIRST or i % 2 == 0):
                 stage_mm(i + 2)
             if i == G_FIRST + 1:

@@ -271,9 +271,12 @@ def tile_fr_pa_kernel(tc, x1, x2, c1_w, c1_b, c2_w, c2_b, out_0, out_1):
             prod[g] = work.tile([P, POS], F32, name="prod%d" % g, tag="prod")
             nc.gpsimd.tensor_tensor(out=prod[g][:], in0=etile[g][:], in1=ysb[g][:, 0:POS], op=ALU.mult)
 
+        def slot(g):
+            return ((g - G_FIRST) // 2 + 1) % BATCH
+
         def stage_fold(g):
-            q = ((g - G_FIRST) // 2) % BATCH
-            if q == 0:
+            q = slot(g)
+            if q == 0 or g == G_FIRST:
                 acc[0] = bank(6, "acc%d" % g)
             for blk in range(POS // P):
                 nc.tensor.matmul(
@@ -286,10 +289,12 @@ def tile_fr_pa_kernel(tc, x1, x2, c1_w, c1_b, c2_w, c2_b, out_0, out_1):
                 )
 
         def stage_finish(last):
+            hi = slot(last)
+            lo = max(0, hi - (last - G_FIRST) // 2)
             accsb = work.tile([P, BATCH * P], F32, name="accsb%d" % last, tag="accsb", bufs=2)
-            nc.vector.tensor_copy(out=accsb[:], in_=acc[0][:])
-            for q in range(BATCH):
-                k = column(last - 2 * (BATCH - 1 - q))
+            nc.vector.tensor_copy(out=accsb[:, lo * P : (hi + 1) * P], in_=acc[0][:, lo * P : (hi + 1) * P])
+            for q in range(lo, hi + 1):
+                k = column(last - 2 * (hi - q))
                 nc.tensor.matmul(
                     out=fin[:, k : k + 1], lhsT=accsb[:, q * P : (q + 1) * P], rhs=ones[:], start=True, stop=True
                 )
@@ -359,7 +364,7 @@ def tile_fr_pa_kernel(tc, x1, x2, c1_w, c1_b, c2_w, c2_b, out_0, out_1):
             if i == G_FIRST + 1:
                 fin = bank(7, "fin")
                 nc.tensor.matmul(out=fin[:, 0:NG], lhsT=ident[:], rhs=zeros[:], start=True, stop=True)
-            if is_g(i - 5) and ((i - 5 - G_FIRST) // 2) % BATCH == BATCH - 1:
+            if is_g(i - 5) and (slot(i - 5) == BATCH - 1 or i - 5 == G_LAST):
                 stage_finish(i - 5)
             if is_g(i - 4):
                 stage_fold(i - 4)

from contextlib import ExitStack

import concourse.mybir as mybir
from concourse.masks import make_identity

F32 = mybir.dt.float32
BF16 = mybir.dt.bfloat16
U32 = mybir.dt.uint32
U8 = mybir.dt.uint8
FP8X4 = mybir.dt.float8_e4m3fn_x4
ACT = mybir.ActivationFunctionType
ALU = mybir.AluOpType
AX = mybir.AxisListType

P = 128
PACK = 4
NB = 4
POS = 1024
HALF = 512
NW = 2
OT = 4
NG = NB * NW * OT
RUN = 4
VSHARE = 296
G_FIRST = 5
G_LAST = 27
BATCH = 4


def is_g(g):
    return g % 2 == 1 and G_FIRST <= g <= G_LAST


FLOPS = 2 * NW * NB * 512 * 1024 * 1024


def tile_fr_pa_kernel(tc, x1, x2, c1_w, c1_b, c2_w, c2_b, out_0, out_1):
    nc = tc.nc
    xsrc = (x1, x2)
    with ExitStack() as ctx:
        keep = ctx.enter_context(tc.tile_pool(name="keep", bufs=1))
        work = ctx.enter_context(tc.tile_pool(name="work", bufs=3))
        psum = ctx.enter_context(tc.psum_pool(name="psum", bufs=1))
        ctx.enter_context(tc.manual_schedule())

        def bank(b, name):
            return psum.tile([P, HALF], F32, name=name, tag="bank%d" % b)

        ident = keep.tile([P, P], F32, name="ident")
        make_identity(nc, ident[:])
        warm_in = keep.tile([P, 1], F32, name="warm_in")
        warm_out = keep.tile([P, 1], F32, name="warm_out")
        nc.vector.memset(warm_in[:], 0.0)
        nc.scalar.activation(out=warm_out[:], in_=warm_in[:], func=ACT.Exp)
        braw = keep.tile([8, P], BF16, name="braw")
        bwide = keep.tile([P, P], F32, name="bwide")
        nc.vector.memset(bwide[:], 0.0)
        result = keep.tile([P, P], F32, name="result")
        nc.vector.memset(result[:], 0.0)
        negm = {}
        sume = keep.tile([P, NG], F32, name="sume")
        sd = keep.tile([P, 2, NG], F32, name="sd")
        nc.vector.memset(sd[:], 0.0)
        zeros = keep.tile([P, NG], F32, name="zeros")
        nc.vector.memset(zeros[:], 0.0)
        ones = keep.tile([P, 1], F32, name="ones")
        nc.vector.memset(ones[:], 1.0)
        junk = keep.tile([P, HALF], F32, name="junk")
        rec = keep.tile([P, NG], F32, name="rec")

        wraw0 = keep.tile([P, 2, 1024], BF16, name="wraw0")
        wraw1 = keep.tile([P, 2, 1024], BF16, name="wraw1")
        wraw2 = keep.tile([P, 4, 1024], BF16, name="wraw2")
        xraw = {}

        def load_x(n, c):
            t = work.tile([P, PACK, POS], BF16, name="xraw%d%d" % (n, c), tag="xraw", bufs=6)
            nc.sync.dma_start(out=t[:], in_=xsrc[c][n].rearrange("(p j) h w -> p j (h w)", j=PACK))
            xraw[(n, c)] = t

        nc.sync.dma_start(out=braw[0:4, :], in_=c1_b.rearrange("(t p) -> t p", p=P))
        nc.sync.dma_start(out=braw[4:8, :], in_=c2_b.rearrange("(t p) -> t p", p=P))
        load_x(0, 0)
        nc.sync.dma_start(out=wraw0[:], in_=c1_w[0:256, :].rearrange("(t p) k -> p t k", p=P))
        load_x(0, 1)
        nc.sync.dma_start(out=wraw1[:], in_=c1_w[256:512, :].rearrange("(t p) k -> p t k", p=P))
        nc.sync.dma_start(out=wraw2[:], in_=c2_w.rearrange("(t p) k -> p t k", p=P))
        for n in range(1, NB - 1):
            load_x(n, 0)
            load_x(n, 1)

        def wrow(j):
            if j < 2:
                return wraw0[:, j, :].bitcast(F32)
            if j < 4:
                return wraw1[:, j - 2, :].bitcast(F32)
            return wraw2[:, j - 4, :].bitcast(F32)

        wq = {}
        ws = {}

        def transpose_w(tiles, banks):
            turned = []
            for j, b in zip(tiles, banks):
                words = wrow(j)
                wt = bank(b, "wt%d" % j)
                for c in range(2):
                    for u in range(2):
                        q = 2 * c + u
                        nc.tensor.transpose(
                            out=wt[:, q * P : (q + 1) * P],
                            in_=words[:, 256 * c + u : 256 * c + 256 : 2],
                            identity=ident[:],
                        )
                turned.append(wt)
            return tiles, turned

        def finish_w(prepared):
            tiles, turned = prepared
            nt = len(tiles)
            gw = work.tile([P, nt * 1024], BF16, name="gw%d" % tiles[0], tag="gw", bufs=2, align_bytes=64)
            codes = keep.tile([P, nt * 256], U32, name="wq%d" % tiles[0], align_bytes=64)
            plane = keep.tile([P, nt * 256], U8, name="ws%d" % tiles[0], align_bytes=64)
            for i, j in enumerate(tiles):
                nc.scalar.copy(
                    out=gw[:, i * 1024 : (i + 1) * 1024].bitcast(F32).rearrange("p (c o u) -> p c o u", c=2, u=2),
                    in_=turned[i][:].rearrange("p (c u o) -> p c o u", c=2, u=2),
                )
                wq[j] = codes[:, i * 256 : (i + 1) * 256]
                ws[j] = plane[:, i * 256 : (i + 1) * 256]
            nc.vector.quantize_mx(out=codes[:].bitcast(FP8X4), scales=plane[:], in_=gw[:])

        bias = keep.tile([P, 8], F32, name="bias")

        def prep_bias():
            bt = bank(2, "bt")
            nc.tensor.transpose(out=bt[:, 0:P], in_=bwide[:], identity=ident[:])
            nc.vector.tensor_copy(out=bias[:], in_=bt[:, 0:8])

        xq = {}
        xs = {}
        xg = {}

        def new_x(n):
            xg[n] = work.tile([P, 2, POS, PACK], BF16, name="xg%d" % n, tag="xg", bufs=2, align_bytes=64)
            xq[n] = keep.tile([P, 2, POS], U32, name="xq%d" % n, align_bytes=64)
            xs[n] = keep.tile([P, 2, POS], U8, name="xs%d" % n, align_bytes=64)

        def views(n, c, lo, hi):
            dst = xg[n][:, c, lo:hi, :].rearrange("p (q i) t -> p q t i", i=RUN)
            src = xraw[(n, c)][:, :, lo:hi].rearrange("p t (q i) -> p q t i", i=RUN)
            return dst, src

        def quant_x(n, c, lo, hi):
            nc.vector.quantize_mx(
                out=xq[n][:, c, lo:hi].bitcast(FP8X4),
                scales=xs[n][:, c, lo:hi],
                in_=xg[n][:, c, lo:hi, :].rearrange("p w t -> p (w t)"),
            )

        def regroup_head(c):
            for h in range(2):
                dst, src = views(0, c, h * HALF, h * HALF + VSHARE)
                nc.vector.tensor_copy(out=dst, in_=src)
                dst, src = views(0, c, h * HALF + VSHARE, (h + 1) * HALF)
                nc.scalar.copy(out=dst, in_=src)

        def regroup_gpsimd(n, c, h):
            nc.gpsimd.tensor_scalar(
                out=xg[n][:, c, h * HALF : (h + 1) * HALF, :],
                in0=xraw[(n, c)][:, :, h * HALF : (h + 1) * HALF].rearrange("p t w -> p w t"),
                scalar1=1.0,
                scalar2=0.0,
                op0=ALU.mult,
                op1=ALU.add,
            )

        ybank = {}
        ysb = {}
        prod = {}
        acc = {}
        atile = {}
        etile = {}

        def column(g):
            n, j = divmod(g, 8)
            return (j // OT) * (NB * OT) + n * OT + j % OT

        def stage_mm(g):
            n, j = divmod(g, 8)
            if g < 4:
                pair = g
            elif g == NG - 1:
                pair = 1
            elif g % 2 == 1 and g >= G_FIRST:
                pair = 0
            else:
                pair = (1, 0, 2, 3)[g % 4]
            ybank[g] = [bank(2 * pair + h, "y%d_%d" % (g, h)) for h in range(2)]
            for h in range(2):
                for c in range(2):
                    nc.tensor.matmul_mx(
                        out=ybank[g][h][:],
                        lhsT=wq[j][:, c * P : (c + 1) * P].bitcast(FP8X4),
                        lhsT_scale=ws[j][:, c * P : (c + 1) * P],
                        rhs=xq[n][:, c, h * HALF : (h + 1) * HALF].bitcast(FP8X4),
                        rhs_scale=xs[n][:, c, h * HALF : (h + 1) * HALF],
                        start=(c == 0),
                        stop=(c == 1),
                    )

        def stage_copy_max(g):
            ysb[g] = work.tile([P, POS + 2], F32, name="ysb%d" % g, tag="ysb", bufs=4)
            for h in range(2):
                nc.vector.tensor_scalar(
                    out=ysb[g][:, h * HALF : (h + 1) * HALF],
                    in0=ybank[g][h][:],
                    scalar1=1.0,
                    scalar2=None,
                    op0=ALU.mult,
                    op1=ALU.max,
                    accum_out=ysb[g][:, POS + h : POS + h + 1],
                )

        def stage_a(g):
            j = g % 8
            atile[g] = work.tile([P, POS + 2], F32, name="a%d" % g, tag="a")
            if is_g(g):
                nc.scalar.activation(out=atile[g][:], in_=ysb[g][:], func=ACT.Exp, bias=bias[:, j : j + 1], scale=1.0)
                return
            for h in range(2):
                nc.scalar.activation(
                    out=atile[g][:, h * HALF : (h + 1) * HALF],
                    in_=ybank[g][h][:],
                    func=ACT.Exp,
                    bias=bias[:, j : j + 1],
                    scale=1.0,
                )

        def stage_b(g):
            negm[g] = work.tile([P, 1], F32, name="negm%d" % g, tag="negm", bufs=4)
            src = atile[g][:, POS : POS + 2] if is_g(g) else atile[g][:, 0:POS]
            nc.vector.tensor_reduce(out=negm[g][:], in_=src, axis=AX.X, op=ALU.max, negate=True)

        def stage_c(g):
            k = column(g)
            etile[g] = work.tile([P, POS], F32, name="e%d" % g, tag="e")
            nc.scalar.activation(
                out=etile[g][:],
                in_=atile[g][:, 0:POS],
                func=ACT.Exp,
                bias=negm[g][:],
                scale=1.0,
                accum_out=sume[:, k : k + 1],
            )

        def stage_d(g):
            k = column(g)
            for h in range(2):
                nc.vector.scalar_tensor_tensor(
                    out=junk[:],
                    in0=ybank[g][h][:],
                    scalar=1.0,
                    in1=etile[g][:, h * HALF : (h + 1) * HALF],
                    op0=ALU.mult,
                    op1=ALU.mult,
                    accum_out=sd[:, h, k : k + 1],
                )

        def stage_prod(g):
            prod[g] = work.tile([P, POS], F32, name="prod%d" % g, tag="prod")
            nc.gpsimd.tensor_tensor(out=prod[g][:], in0=etile[g][:], in1=ysb[g][:, 0:POS], op=ALU.mult)

        def slot(g):
            return ((g - G_FIRST) // 2 + 1) % BATCH

        def stage_fold(g):
            q = slot(g)
            if q == 0 or g == G_FIRST:
                acc[0] = bank(6, "acc%d" % g)
            for blk in range(POS // P):
                nc.tensor.matmul(
                    out=acc[0][:, q * P : (q + 1) * P],
                    lhsT=prod[g][:, blk * P : (blk + 1) * P],
                    rhs=ident[:],
                    is_transpose=True,
                    start=(blk == 0),
                    stop=(blk == POS // P - 1),
                )

        def stage_finish(last):
            hi = slot(last)
            lo = max(0, hi - (last - G_FIRST) // 2)
            accsb = work.tile([P, BATCH * P], F32, name="accsb%d" % last, tag="accsb", bufs=2)
            nc.vector.tensor_copy(out=accsb[:, lo * P : (hi + 1) * P], in_=acc[0][:, lo * P : (hi + 1) * P])
            for q in range(lo, hi + 1):
                k = column(last - 2 * (hi - q))
                nc.tensor.matmul(
                    out=fin[:, k : k + 1], lhsT=accsb[:, q * P : (q + 1) * P], rhs=ones[:], start=True, stop=True
                )

        new_x(0)
        nc.vector.tensor_copy(out=bwide[0:8, :], in_=braw[:])
        regroup_head(0)
        quant_x(0, 0, 0, HALF)
        quant_x(0, 0, HALF, POS)
        finish_w(transpose_w([0, 1], [0, 1]))
        prep_bias()
        regroup_head(1)
        quant_x(0, 1, 0, HALF)
        quant_x(0, 1, HALF, POS)
        finish_w(transpose_w([2, 3], [4, 5]))
        stage_mm(0)
        stage_mm(1)
        late_w = {2: transpose_w([4, 5], [6, 7])}
        stage_mm(2)
        load_x(NB - 1, 0)
        load_x(NB - 1, 1)
        new_x(1)
        for c in range(2):
            for h in range(2):
                regroup_gpsimd(1, c, h)
        pieces = [(n, c, h) for n in range(2, NB) for c in range(2) for h in range(2)]

        fin = None
        for i in range(NG + 2):
            if is_g(i + 2) and i + 2 > G_FIRST:
                stage_copy_max(i + 2)
            if i >= 2:
                stage_c(i - 2)
                if i - 2 == NG - 1:
                    nc.vector.reciprocal(out=rec[:], in_=sume[:])
                if is_g(i - 2):
                    stage_prod(i - 2)
                else:
                    stage_d(i - 2)
            if i == NG - 2:
                stage_mm(NG - 1)
            if i in late_w:
                finish_w(late_w[i])
            if i == G_FIRST - 2:
                stage_mm(G_FIRST)
            if i < NG:
                stage_a(i)
                stage_b(i)
            if i == G_FIRST - 2:
                stage_copy_max(G_FIRST)
            if i % 8 in (3, 5) and i // 8 + 1 < NB:
                quant_x(i // 8 + 1, (i % 8 - 3) // 2, 0, POS)
            if i % 2 == 0 and 0 <= (i - 4) // 2 < len(pieces):
                n, c, h = pieces[(i - 4) // 2]
                if c == 0 and h == 0:
                    new_x(n)
                regroup_gpsimd(n, c, h)
            if i == 2:
                stage_mm(3)
                late_w[3] = transpose_w([6, 7], [0, 1])
            if i == 3:
                stage_mm(4)
            if i % 2 == 0 and G_FIRST < i + 3 < NG - 1:
                stage_mm(i + 3)
            if 3 <= i < NG - 2 and (i + 2 < G_FIRST or i % 2 == 0):
                stage_mm(i + 2)
            if i == G_FIRST + 1:
                fin = bank(7, "fin")
                nc.tensor.matmul(out=fin[:, 0:NG], lhsT=ident[:], rhs=zeros[:], start=True, stop=True)
            if is_g(i - 5) and (slot(i - 5) == BATCH - 1 or i - 5 == G_LAST):
                stage_finish(i - 5)
            if is_g(i - 4):
                stage_fold(i - 4)

        num = keep.tile([P, NG], F32, name="num")
        nc.vector.tensor_add(out=num[:], in0=sd[:, 0, :], in1=sd[:, 1, :])
        nc.vector.tensor_add(out=num[:], in0=num[:], in1=fin[:, 0:NG])
        nc.vector.tensor_mul(out=num[:], in0=num[:], in1=rec[:])
        nc.vector.tensor_add(
            out=result[:, 0:NG].rearrange("p (w n t) -> p w n t", w=NW, n=NB),
            in0=num[:].rearrange("p (w n t) -> p w n t", w=NW, n=NB),
            in1=bias[:].rearrange("p (w t) -> p w t", w=NW).unsqueeze(2).to_broadcast([P, NW, NB, OT]),
        )
        rt = bank(0, "rt")
        nc.tensor.transpose(out=rt[:, 0:P], in_=result[:], identity=ident[:])
        rows = keep.tile([P, P], F32, name="rows")
        nc.vector.tensor_copy(out=rows[:], in_=rt[:, 0:P])
        nc.sync.dma_start(out=out_0.rearrange("n (t p) -> (n t) p", p=P), in_=rows[0:16, :])
        nc.sync.dma_start(out=out_1.rearrange("n (t p) -> (n t) p", p=P), in_=rows[16:32, :])
